import numpy as np
import ml_dtypes


def mxq(x, axis, fmt="e4m3"):
    dtype, down = {"e4m3": (ml_dtypes.float8_e4m3fn, 7), "e5m2": (ml_dtypes.float8_e5m2, 14)}[fmt]
    v = np.moveaxis(np.asarray(x, np.float32).astype(ml_dtypes.bfloat16).astype(np.float64), axis, -1)
    blocks = v.reshape(v.shape[:-1] + (-1, 32))
    amax = np.abs(blocks).max(-1, keepdims=True)
    byte = np.maximum(np.where(amax > 0, np.frexp(amax)[1] - 1 + 127, 0) - down, 1)
    scale = np.exp2(byte - 127.0)
    codes = (blocks / scale).astype(np.float32).astype(dtype).astype(np.float64)
    return np.moveaxis((codes * scale).reshape(v.shape), -1, axis)


WIDE = False


def mx_kscale(k):
    if not WIDE:
        return np.ones(k)
    levels = np.array([10, -10, 5, -5, 0])
    a = np.random.permutation(np.resize(levels, k // 512 * 4)).reshape(k // 512, 4)
    idx = np.arange(k)
    return np.exp2(a[idx // 512, idx % 128 // 32])


BF16 = ml_dtypes.bfloat16


def bf(x):
    return np.asarray(x, np.float32).astype(BF16)


def f64(x):
    return np.asarray(x).astype(np.float64)


N, L, E, H, D = 4, 256, 1024, 16, 64
HD = H * D


def setup_inputs():
    s = mx_kscale(E)
    g = (E / D) ** 0.25 / np.sqrt(E)
    return {"x": bf(np.random.standard_normal((N, L, E)) * s),
            "Wq": bf(np.random.standard_normal((E, HD)) * g / s[:, None]),
            "Wk": bf(np.random.standard_normal((E, HD)) * g / s[:, None])}


def reference(x, Wq, Wk):
    xq = mxq(f64(x), 2, "e4m3")
    q = (xq @ mxq(f64(Wq), 0, "e4m3")).reshape(N, L, H, D)
    k = (xq @ mxq(f64(Wk), 0, "e4m3")).reshape(N, L, H, D)
    energy = np.stack([(q * k[:, :, j:j + 1, :]).sum(-1) for j in range(H)], axis=-1)
    sc = energy / np.sqrt(E)
    e = np.exp(sc - sc.max(-1, keepdims=True))
    return e / e.sum(-1, keepdims=True)

@@ -1,0 +1,223 @@
+import math
+
+import concourse.mybir as mybir
+from concourse.masks import make_identity
+
+F32 = mybir.dt.float32
+BF16 = mybir.dt.bfloat16
+I32 = mybir.dt.int32
+U32 = mybir.dt.uint32
+U8 = mybir.dt.uint8
+FP8X4 = mybir.dt.float8_e4m3fn_x4
+ALU = mybir.AluOpType
+ACT = mybir.ActivationFunctionType
+AXIS_X = mybir.AxisListType.X
+
+P = 128
+PACK = 4
+K_PASS = P * PACK
+TOKENS = 4 * 256
+E = 1024
+HEADS = 16
+D = 64
+PASSES = E // K_PASS
+SLOTS = 2
+PAIRS = TOKENS // SLOTS
+BLOCK_PAIRS = P
+BLOCKS = PAIRS // BLOCK_PAIRS
+GROUP_PAIRS = P // (SLOTS * HEADS)
+GROUPS = PAIRS // GROUP_PAIRS
+BLOCK_GROUPS = GROUPS // BLOCKS
+GROUP_COLS = HEADS * GROUP_PAIRS
+BANK_F32 = 512
+BANK_GROUPS = BANK_F32 // GROUP_COLS
+QUAD = BANK_F32 // BLOCK_PAIRS
+HALF_COLS = 512
+HALF_HEADS = HALF_COLS // D
+W_SLOTTED = (2 * HEADS + 1) * D
+
+FLOPS = 2 * 2 * TOKENS * E * HEADS * D + 2 * TOKENS * HEADS * HEADS * D
+
+
+def head_window(head, slot):
+    first = (2 * head + 1 - slot) * D
+    return slice(first, first + P)
+
+
+def tile_multiheadattention_pa_kernel(tc, x, Wq, Wk, out):
+    nc = tc.nc
+    x_blocks = x.flatten_outer_dims().rearrange("(b p s) e -> s b p e", p=P, s=SLOTS)
+    out_rows = out.rearrange("n l i j -> (n l i) j").rearrange("(g p) j -> p g j", p=P)
+
+    with (
+        tc.tile_pool(name="keep", bufs=1) as keep,
+        tc.tile_pool(name="x_in", bufs=SLOTS * BLOCKS) as x_in,
+        tc.tile_pool(name="w_in", bufs=4) as w_in,
+        tc.tile_pool(name="w_stage", bufs=3) as w_stage,
+        tc.tile_pool(name="q_pool", bufs=2) as q_pool,
+        tc.tile_pool(name="soft", bufs=2) as soft,
+        tc.psum_pool(name="mx_psum", bufs=5) as mx_psum,
+        tc.psum_pool(name="e_psum", bufs=3) as e_psum,
+        tc.manual_schedule(),
+    ):
+        identity = keep.tile([P, P], F32)
+        make_identity(nc, identity[:])
+
+        x_grouped = keep.tile([P, PASSES, SLOTS, PAIRS * PACK], BF16, align_bytes=64)
+        x_codes = keep.tile([P, PASSES, SLOTS, PAIRS], U32, align_bytes=64)
+        x_scales = keep.tile([P, PASSES, SLOTS, PAIRS], U8, align_bytes=64)
+        wk_codes = keep.tile([P, PASSES, W_SLOTTED], U32, align_bytes=64)
+        wk_scales = keep.tile([P, PASSES, W_SLOTTED], U8, align_bytes=64)
+        wq_codes = keep.tile([P, PASSES, W_SLOTTED], U32, align_bytes=64)
+        wq_scales = keep.tile([P, PASSES, W_SLOTTED], U8, align_bytes=64)
+        k_moving = keep.tile([P, GROUPS, HEADS, GROUP_PAIRS], F32)
+
+        for codes, scales in ((wk_codes, wk_scales), (wq_codes, wq_scales)):
+            code_runs = codes[:].bitcast(I32).rearrange("p c (r w) -> p c r w", w=D)
+            scale_runs = scales[:].bitcast(I32).rearrange("p c (r w) -> p c r w", w=D // 4)
+            nc.vector.memset(code_runs[:, :, 0 : 2 * HEADS + 1 : 2, :], 0)
+            nc.vector.memset(scale_runs[:, :, 0 : 2 * HEADS + 1 : 2, :], 0)
+
+        x_words = x_grouped[:].bitcast(F32).rearrange("p c s (v h) -> p c s v h", h=2)
+        for slot in range(SLOTS):
+            for block in range(BLOCKS):
+                pairs = slice(block * BLOCK_PAIRS, (block + 1) * BLOCK_PAIRS)
+                x_raw = x_in.tile([P, E], BF16)
+                nc.sync.dma_start(out=x_raw[:], in_=x_blocks[slot, block])
+                x_t = mx_psum.tile([P, PASSES * 2, BLOCK_PAIRS], F32, tag="bank")
+                for plane in range(PASSES * 2):
+                    nc.tensor.transpose(
+                        x_t[:, plane, :],
+                        x_raw[:].bitcast(F32)[:, plane * P : (plane + 1) * P],
+                        identity[:],
+                    )
+                nc.scalar.copy(
+                    out=x_words[:, :, slot, pairs, :],
+                    in_=x_t[:].rearrange("p (c h) v -> p c v h", h=2),
+                )
+                for c in range(PASSES):
+                    nc.vector.quantize_mx(
+                        out=x_codes[:, c, slot, pairs].bitcast(FP8X4),
+                        scales=x_scales[:, c, slot, pairs],
+                        in_=x_grouped[:, c, slot, block * BLOCK_PAIRS * PACK : (block + 1) * BLOCK_PAIRS * PACK],
+                    )
+
+        def quantise_weight(w, codes, scales):
+            for half in range(HEADS // HALF_HEADS):
+                cols = slice(half * HALF_COLS, (half + 1) * HALF_COLS)
+                w_raw = w_in.tile([P, PASSES, PACK, HALF_COLS], BF16)
+                for c in range(PASSES):
+                    for h in range(2):
+                        first = c * K_PASS + h * 2 * P
+                        nc.sync.dma_start(
+                            out=w_raw[:, c, 2 * h : 2 * h + 2, :],
+                            in_=w[first : first + 2 * P, cols].rearrange("(p r) n -> p r n", r=2),
+                        )
+                grouped = []
+                for c in range(PASSES):
+                    w_grouped = w_stage.tile([P, HALF_COLS, PACK], BF16, align_bytes=64)
+                    nc.vector.tensor_copy(
+                        out=w_grouped[:].rearrange("p (n i) t -> p n t i", i=4),
+                        in_=w_raw[:, c].rearrange("p t (n i) -> p n t i", i=4),
+                    )
+                    grouped.append(w_grouped)
+                for c in range(PASSES):
+                    for h in range(HALF_HEADS):
+                        first = (2 * (half * HALF_HEADS + h) + 1) * D
+                        nc.vector.quantize_mx(
+                            out=codes[:, c, first : first + D].bitcast(FP8X4),
+                            scales=scales[:, c, first : first + D],
+                            in_=grouped[c][:, h * D : (h + 1) * D, :].rearrange("p n t -> p (n t)"),
+                        )
+
+        quantise_weight(Wk, wk_codes, wk_scales)
+        quantise_weight(Wq, wq_codes, wq_scales)
+
+        for head in range(HEADS):
+            k_bank = mx_psum.tile([P, PAIRS], F32, tag="bank")
+            for slot in range(SLOTS):
+                for c in range(PASSES):
+                    nc.tensor.matmul_mx(
+                        out=k_bank[:],
+                        lhsT=wk_codes[:, c, head_window(head, slot)].bitcast(FP8X4),
+                        lhsT_scale=wk_scales[:, c, head_window(head, slot)],
+                        rhs=x_codes[:, c, slot, :].bitcast(FP8X4),
+                        rhs_scale=x_scales[:, c, slot, :],
+                        start=(slot == 0 and c == 0),
+                        stop=(slot == SLOTS - 1 and c == PASSES - 1),
+                    )
+            nc.scalar.copy(
+                out=k_moving[:, :, head, :],
+                in_=k_bank[:].rearrange("p (g v) -> p g v", v=GROUP_PAIRS),
+            )
+
+        def project_q(block):
+            pairs = slice(block * BLOCK_PAIRS, (block + 1) * BLOCK_PAIRS)
+            q_stationary = q_pool.tile([P, BLOCK_PAIRS, SLOTS, HEADS], F32)
+            for slot in range(SLOTS):
+                for quad in range(HEADS // QUAD):
+                    q_bank = mx_psum.tile([P, QUAD, BLOCK_PAIRS], F32, tag="bank")
+                    for i in range(QUAD):
+                        head = quad * QUAD + i
+                        for c in range(PASSES):
+                            nc.tensor.matmul_mx(
+                                out=q_bank[:, i, :],
+                                lhsT=wq_codes[:, c, head_window(head, slot)].bitcast(FP8X4),
+                                lhsT_scale=wq_scales[:, c, head_window(head, slot)],
+                                rhs=x_codes[:, c, slot, pairs].bitcast(FP8X4),
+                                rhs_scale=x_scales[:, c, slot, pairs],
+                                start=(c == 0),
+                                stop=(c == PASSES - 1),
+                            )
+                    nc.scalar.copy(
+                        out=q_stationary[:, :, slot, quad * QUAD : (quad + 1) * QUAD],
+                        in_=q_bank[:].rearrange("p i v -> p v i"),
+                    )
+            return q_stationary
+
+        def attend(block, q_stationary):
+            scores = soft.tile([P, BLOCK_GROUPS, HEADS], F32)
+            for bank in range(BLOCK_GROUPS // BANK_GROUPS):
+                e_bank = e_psum.tile([P, BANK_GROUPS, HEADS, GROUP_PAIRS], F32)
+                for g in range(BANK_GROUPS):
+                    local = bank * BANK_GROUPS + g
+                    nc.tensor.matmul(
+                        out=e_bank[:, g].rearrange("p j v -> p (j v)"),
+                        lhsT=q_stationary[:, local * GROUP_PAIRS : (local + 1) * GROUP_PAIRS].rearrange(
+                            "p u s i -> p (u s i)"
+                        ),
+                        rhs=k_moving[:, block * BLOCK_GROUPS + local].rearrange("p j v -> p (j v)"),
+                        start=True,
+                        stop=True,
+                    )
+                for u in range(GROUP_PAIRS):
+                    rows = slice(u * SLOTS * HEADS, (u + 1) * SLOTS * HEADS)
+                    nc.vector.tensor_copy(
+                        out=scores[rows, bank * BANK_GROUPS : (bank + 1) * BANK_GROUPS, :],
+                        in_=e_bank[rows, :, :, u],
+                    )
+
+            wide = [P, BLOCK_GROUPS, HEADS]
+            top = soft.tile([P, BLOCK_GROUPS], F32)
+            nc.vector.tensor_reduce(out=top[:], in_=scores[:], axis=AXIS_X, op=ALU.max)
+            nc.vector.tensor_tensor(
+                out=scores[:], in0=scores[:], in1=top[:].unsqueeze(2).to_broadcast(wide), op=ALU.subtract
+            )
+            weights = soft.tile([P, BLOCK_GROUPS, HEADS], F32)
+            nc.scalar.activation(out=weights[:], in_=scores[:], func=ACT.Exp, scale=1.0 / math.sqrt(E))
+            total = soft.tile([P, BLOCK_GROUPS], F32)
+            nc.vector.tensor_reduce(out=total[:], in_=weights[:], axis=AXIS_X, op=ALU.add)
+            nc.vector.reciprocal(out=total[:], in_=total[:])
+            nc.vector.tensor_tensor(
+                out=weights[:], in0=weights[:], in1=total[:].unsqueeze(2).to_broadcast(wide), op=ALU.mult
+            )
+            nc.sync.dma_start(
+                out=out_rows[:, block * BLOCK_GROUPS : (block + 1) * BLOCK_GROUPS, :], in_=weights[:]
+            )
+
+        q_next = project_q(0)
+        for block in range(BLOCKS):
+            q_now = q_next
+            if block + 1 < BLOCKS:
+                q_next = project_q(block + 1)
+            attend(block, q_now)

@@ -31,9 +31,13 @@ BLOCK_GROUPS = GROUPS // BLOCKS
 GROUP_COLS = HEADS * GROUP_PAIRS
 BANK_F32 = 512
 BANK_GROUPS = BANK_F32 // GROUP_COLS
+ROUNDS = BLOCK_GROUPS // BANK_GROUPS
+PSUM_BANKS = 8
 QUAD = BANK_F32 // BLOCK_PAIRS
+Q_BANKS = SLOTS * HEADS // QUAD
 HALF_COLS = 512
 HALF_HEADS = HALF_COLS // D
+HALVES = HEADS // HALF_HEADS
 W_SLOTTED = (2 * HEADS + 1) * D
 
 FLOPS = 2 * 2 * TOKENS * E * HEADS * D + 2 * TOKENS * HEADS * HEADS * D
@@ -51,44 +55,49 @@ def tile_multiheadattention_pa_kernel(tc, x, Wq, Wk, out):
 
     with (
         tc.tile_pool(name="keep", bufs=1) as keep,
-        tc.tile_pool(name="x_in", bufs=SLOTS * BLOCKS) as x_in,
-        tc.tile_pool(name="w_in", bufs=4) as w_in,
         tc.tile_pool(name="w_stage", bufs=3) as w_stage,
         tc.tile_pool(name="q_pool", bufs=2) as q_pool,
-        tc.tile_pool(name="soft", bufs=2) as soft,
-        tc.psum_pool(name="mx_psum", bufs=5) as mx_psum,
-        tc.psum_pool(name="e_psum", bufs=3) as e_psum,
+        tc.tile_pool(name="soft", bufs=4) as soft,
+        tc.psum_pool(name="psum", bufs=PSUM_BANKS) as psum,
         tc.manual_schedule(),
     ):
         identity = keep.tile([P, P], F32)
         make_identity(nc, identity[:])
 
+        x_raw = keep.tile([P, SLOTS, BLOCKS, E], BF16)
+        for slot in range(SLOTS):
+            for block in range(BLOCKS):
+                nc.sync.dma_start(out=x_raw[:, slot, block, :], in_=x_blocks[slot, block])
+
+        def load_weight(w, w_raw):
+            for half in range(HALVES):
+                cols = slice(half * HALF_COLS, (half + 1) * HALF_COLS)
+                for c in range(PASSES):
+                    for h in range(2):
+                        first = c * K_PASS + h * 2 * P
+                        nc.sync.dma_start(
+                            out=w_raw[:, half, c, 2 * h : 2 * h + 2, :],
+                            in_=w[first : first + 2 * P, cols].rearrange("(p r) n -> p r n", r=2),
+                        )
+
+        wk_raw = keep.tile([P, HALVES, PASSES, PACK, HALF_COLS], BF16)
+        wq_raw = keep.tile([P, HALVES, PASSES, PACK, HALF_COLS], BF16)
+        load_weight(Wk, wk_raw)
+        load_weight(Wq, wq_raw)
+
         x_grouped = keep.tile([P, PASSES, SLOTS, PAIRS * PACK], BF16, align_bytes=64)
         x_codes = keep.tile([P, PASSES, SLOTS, PAIRS], U32, align_bytes=64)
         x_scales = keep.tile([P, PASSES, SLOTS, PAIRS], U8, align_bytes=64)
-        wk_codes = keep.tile([P, PASSES, W_SLOTTED], U32, align_bytes=64)
-        wk_scales = keep.tile([P, PASSES, W_SLOTTED], U8, align_bytes=64)
-        wq_codes = keep.tile([P, PASSES, W_SLOTTED], U32, align_bytes=64)
-        wq_scales = keep.tile([P, PASSES, W_SLOTTED], U8, align_bytes=64)
-        k_moving = keep.tile([P, GROUPS, HEADS, GROUP_PAIRS], F32)
-
-        for codes, scales in ((wk_codes, wk_scales), (wq_codes, wq_scales)):
-            code_runs = codes[:].bitcast(I32).rearrange("p c (r w) -> p c r w", w=D)
-            scale_runs = scales[:].bitcast(I32).rearrange("p c (r w) -> p c r w", w=D // 4)
-            nc.vector.memset(code_runs[:, :, 0 : 2 * HEADS + 1 : 2, :], 0)
-            nc.vector.memset(scale_runs[:, :, 0 : 2 * HEADS + 1 : 2, :], 0)
-
         x_words = x_grouped[:].bitcast(F32).rearrange("p c s (v h) -> p c s v h", h=2)
         for slot in range(SLOTS):
             for block in range(BLOCKS):
                 pairs = slice(block * BLOCK_PAIRS, (block + 1) * BLOCK_PAIRS)
-                x_raw = x_in.tile([P, E], BF16)
-                nc.sync.dma_start(out=x_raw[:], in_=x_blocks[slot, block])
-                x_t = mx_psum.tile([P, PASSES * 2, BLOCK_PAIRS], F32, tag="bank")
+                values = slice(block * BLOCK_PAIRS * PACK, (block + 1) * BLOCK_PAIRS * PACK)
+                x_t = psum.tile([P, PASSES * 2, BLOCK_PAIRS], F32, tag="bank")
                 for plane in range(PASSES * 2):
                     nc.tensor.transpose(
                         x_t[:, plane, :],
-                        x_raw[:].bitcast(F32)[:, plane * P : (plane + 1) * P],
+                        x_raw[:, slot, block, :].bitcast(F32)[:, plane * P : (plane + 1) * P],
                         identity[:],
                     )
                 nc.scalar.copy(
@@ -99,125 +108,139 @@ def tile_multiheadattention_pa_kernel(tc, x, Wq, Wk, out):
                     nc.vector.quantize_mx(
                         out=x_codes[:, c, slot, pairs].bitcast(FP8X4),
                         scales=x_scales[:, c, slot, pairs],
-                        in_=x_grouped[:, c, slot, block * BLOCK_PAIRS * PACK : (block + 1) * BLOCK_PAIRS * PACK],
+                        in_=x_grouped[:, c, slot, values],
                     )
 
-        def quantise_weight(w, codes, scales):
-            for half in range(HEADS // HALF_HEADS):
-                cols = slice(half * HALF_COLS, (half + 1) * HALF_COLS)
-                w_raw = w_in.tile([P, PASSES, PACK, HALF_COLS], BF16)
-                for c in range(PASSES):
-                    for h in range(2):
-                        first = c * K_PASS + h * 2 * P
-                        nc.sync.dma_start(
-                            out=w_raw[:, c, 2 * h : 2 * h + 2, :],
-                            in_=w[first : first + 2 * P, cols].rearrange("(p r) n -> p r n", r=2),
-                        )
+        def quantise_weight(w_raw, codes, scales):
+            code_runs = codes[:].bitcast(I32).rearrange("p c (r w) -> p c r w", w=D)
+            scale_runs = scales[:].bitcast(I32).rearrange("p c (r w) -> p c r w", w=D // 4)
+            nc.vector.memset(code_runs[:, :, 0 : 2 * HEADS + 1 : 2, :], 0)
+            nc.vector.memset(scale_runs[:, :, 0 : 2 * HEADS + 1 : 2, :], 0)
+            for half in range(HALVES):
                 grouped = []
                 for c in range(PASSES):
                     w_grouped = w_stage.tile([P, HALF_COLS, PACK], BF16, align_bytes=64)
                     nc.vector.tensor_copy(
                         out=w_grouped[:].rearrange("p (n i) t -> p n t i", i=4),
-                        in_=w_raw[:, c].rearrange("p t (n i) -> p n t i", i=4),
+                        in_=w_raw[:, half, c].rearrange("p t (n i) -> p n t i", i=4),
                     )
                     grouped.append(w_grouped)
-                for c in range(PASSES):
-                    for h in range(HALF_HEADS):
-                        first = (2 * (half * HALF_HEADS + h) + 1) * D
+                for h in range(HALF_HEADS):
+                    first = (2 * (half * HALF_HEADS + h) + 1) * D
+                    for c in range(PASSES):
                         nc.vector.quantize_mx(
                             out=codes[:, c, first : first + D].bitcast(FP8X4),
                             scales=scales[:, c, first : first + D],
                             in_=grouped[c][:, h * D : (h + 1) * D, :].rearrange("p n t -> p (n t)"),
                         )
 
-        quantise_weight(Wk, wk_codes, wk_scales)
-        quantise_weight(Wq, wq_codes, wq_scales)
+        wk_codes = keep.tile([P, PASSES, W_SLOTTED], U32, align_bytes=64)
+        wk_scales = keep.tile([P, PASSES, W_SLOTTED], U8, align_bytes=64)
+        wq_codes = keep.tile([P, PASSES, W_SLOTTED], U32, align_bytes=64)
+        wq_scales = keep.tile([P, PASSES, W_SLOTTED], U8, align_bytes=64)
+        quantise_weight(wk_raw, wk_codes, wk_scales)
+        quantise_weight(wq_raw, wq_codes, wq_scales)
 
+        k_moving = keep.tile([P, GROUPS, HEADS, GROUP_PAIRS], F32)
         for head in range(HEADS):
-            k_bank = mx_psum.tile([P, PAIRS], F32, tag="bank")
-            for slot in range(SLOTS):
-                for c in range(PASSES):
+            k_bank = psum.tile([P, PAIRS], F32, tag="bank")
+            for c in range(PASSES):
+                for slot in range(SLOTS):
                     nc.tensor.matmul_mx(
                         out=k_bank[:],
                         lhsT=wk_codes[:, c, head_window(head, slot)].bitcast(FP8X4),
                         lhsT_scale=wk_scales[:, c, head_window(head, slot)],
                         rhs=x_codes[:, c, slot, :].bitcast(FP8X4),
                         rhs_scale=x_scales[:, c, slot, :],
-                        start=(slot == 0 and c == 0),
-                        stop=(slot == SLOTS - 1 and c == PASSES - 1),
+                        start=(c == 0 and slot == 0),
+                        stop=(c == PASSES - 1 and slot == SLOTS - 1),
                     )
             nc.scalar.copy(
                 out=k_moving[:, :, head, :],
                 in_=k_bank[:].rearrange("p (g v) -> p g v", v=GROUP_PAIRS),
             )
 
-        def project_q(block):
-            pairs = slice(block * BLOCK_PAIRS, (block + 1) * BLOCK_PAIRS)
+        def new_q():
             q_stationary = q_pool.tile([P, BLOCK_PAIRS, SLOTS, HEADS], F32)
-            for slot in range(SLOTS):
-                for quad in range(HEADS // QUAD):
-                    q_bank = mx_psum.tile([P, QUAD, BLOCK_PAIRS], F32, tag="bank")
-                    for i in range(QUAD):
-                        head = quad * QUAD + i
-                        for c in range(PASSES):
-                            nc.tensor.matmul_mx(
-                                out=q_bank[:, i, :],
-                                lhsT=wq_codes[:, c, head_window(head, slot)].bitcast(FP8X4),
-                                lhsT_scale=wq_scales[:, c, head_window(head, slot)],
-                                rhs=x_codes[:, c, slot, pairs].bitcast(FP8X4),
-                                rhs_scale=x_scales[:, c, slot, pairs],
-                                start=(c == 0),
-                                stop=(c == PASSES - 1),
-                            )
-                    nc.scalar.copy(
-                        out=q_stationary[:, :, slot, quad * QUAD : (quad + 1) * QUAD],
-                        in_=q_bank[:].rearrange("p i v -> p v i"),
-                    )
             return q_stationary
 
-        def attend(block, q_stationary):
-            scores = soft.tile([P, BLOCK_GROUPS, HEADS], F32)
-            for bank in range(BLOCK_GROUPS // BANK_GROUPS):
-                e_bank = e_psum.tile([P, BANK_GROUPS, HEADS, GROUP_PAIRS], F32)
-                for g in range(BANK_GROUPS):
-                    local = bank * BANK_GROUPS + g
-                    nc.tensor.matmul(
-                        out=e_bank[:, g].rearrange("p j v -> p (j v)"),
-                        lhsT=q_stationary[:, local * GROUP_PAIRS : (local + 1) * GROUP_PAIRS].rearrange(
-                            "p u s i -> p (u s i)"
-                        ),
-                        rhs=k_moving[:, block * BLOCK_GROUPS + local].rearrange("p j v -> p (j v)"),
-                        start=True,
-                        stop=True,
+        def project_q(block, bank, q_stationary):
+            slot, quad = divmod(bank, HEADS // QUAD)
+            pairs = slice(block * BLOCK_PAIRS, (block + 1) * BLOCK_PAIRS)
+            q_bank = psum.tile([P, QUAD, BLOCK_PAIRS], F32, tag="bank")
+            for i in range(QUAD):
+                head = quad * QUAD + i
+                for c in range(PASSES):
+                    nc.tensor.matmul_mx(
+                        out=q_bank[:, i, :],
+                        lhsT=wq_codes[:, c, head_window(head, slot)].bitcast(FP8X4),
+                        lhsT_scale=wq_scales[:, c, head_window(head, slot)],
+                        rhs=x_codes[:, c, slot, pairs].bitcast(FP8X4),
+                        rhs_scale=x_scales[:, c, slot, pairs],
+                        start=(c == 0),
+                        stop=(c == PASSES - 1),
                     )
-                for u in range(GROUP_PAIRS):
-                    rows = slice(u * SLOTS * HEADS, (u + 1) * SLOTS * HEADS)
-                    nc.vector.tensor_copy(
-                        out=scores[rows, bank * BANK_GROUPS : (bank + 1) * BANK_GROUPS, :],
-                        in_=e_bank[rows, :, :, u],
-                    )
+            nc.scalar.copy(
+                out=q_stationary[:, :, slot, quad * QUAD : (quad + 1) * QUAD],
+                in_=q_bank[:].rearrange("p i v -> p v i"),
+            )
 
-            wide = [P, BLOCK_GROUPS, HEADS]
-            top = soft.tile([P, BLOCK_GROUPS], F32)
+        wide = [P, BANK_GROUPS, HEADS]
+
+        def shifted_scores(block, r, q_stationary):
+            e_bank = psum.tile([P, BANK_GROUPS, HEADS, GROUP_PAIRS], F32, tag="bank")
+            for g in range(BANK_GROUPS):
+                local = r * BANK_GROUPS + g
+                nc.tensor.matmul(
+                    out=e_bank[:, g].rearrange("p j v -> p (j v)"),
+                    lhsT=q_stationary[:, local * GROUP_PAIRS : (local + 1) * GROUP_PAIRS].rearrange(
+                        "p u s i -> p (u s i)"
+                    ),
+                    rhs=k_moving[:, block * BLOCK_GROUPS + local].rearrange("p j v -> p (j v)"),
+                    start=True,
+                    stop=True,
+                )
+            scores = soft.tile(wide, F32)
+            for u in range(GROUP_PAIRS):
+                rows = slice(u * SLOTS * HEADS, (u + 1) * SLOTS * HEADS)
+                if u % 2 == 0:
+                    nc.scalar.copy(out=scores[rows, :, :], in_=e_bank[rows, :, :, u])
+                else:
+                    nc.vector.tensor_copy(out=scores[rows, :, :], in_=e_bank[rows, :, :, u])
+            top = soft.tile([P, BANK_GROUPS], F32)
             nc.vector.tensor_reduce(out=top[:], in_=scores[:], axis=AXIS_X, op=ALU.max)
             nc.vector.tensor_tensor(
                 out=scores[:], in0=scores[:], in1=top[:].unsqueeze(2).to_broadcast(wide), op=ALU.subtract
             )
-            weights = soft.tile([P, BLOCK_GROUPS, HEADS], F32)
+            return scores
+
+        def normalise_and_store(block, r, scores):
+            weights = soft.tile(wide, F32)
             nc.scalar.activation(out=weights[:], in_=scores[:], func=ACT.Exp, scale=1.0 / math.sqrt(E))
-            total = soft.tile([P, BLOCK_GROUPS], F32)
+            total = soft.tile([P, BANK_GROUPS], F32)
             nc.vector.tensor_reduce(out=total[:], in_=weights[:], axis=AXIS_X, op=ALU.add)
             nc.vector.reciprocal(out=total[:], in_=total[:])
             nc.vector.tensor_tensor(
                 out=weights[:], in0=weights[:], in1=total[:].unsqueeze(2).to_broadcast(wide), op=ALU.mult
             )
-            nc.sync.dma_start(
-                out=out_rows[:, block * BLOCK_GROUPS : (block + 1) * BLOCK_GROUPS, :], in_=weights[:]
-            )
+            first = block * BLOCK_GROUPS + r * BANK_GROUPS
+            nc.sync.dma_start(out=out_rows[:, first : first + BANK_GROUPS, :], in_=weights[:])
 
-        q_next = project_q(0)
+        q_next = new_q()
+        for bank in range(Q_BANKS):
+            project_q(0, bank, q_next)
+        unfinished = []
         for block in range(BLOCKS):
             q_now = q_next
             if block + 1 < BLOCKS:
-                q_next = project_q(block + 1)
-            attend(block, q_now)
+                q_next = new_q()
+            for r in range(ROUNDS):
+                if block + 1 < BLOCKS:
+                    for bank in range(r * Q_BANKS // ROUNDS, (r + 1) * Q_BANKS // ROUNDS):
+                        project_q(block + 1, bank, q_next)
+                scores = shifted_scores(block, r, q_now)
+                for earlier in unfinished:
+                    normalise_and_store(*earlier)
+                unfinished = [(block, r, scores)]
+        for earlier in unfinished:
+            normalise_and_store(*earlier)

@@ -5,7 +5,6 @@ from concourse.masks import make_identity
 
 F32 = mybir.dt.float32
 BF16 = mybir.dt.bfloat16
-I32 = mybir.dt.int32
 U32 = mybir.dt.uint32
 U8 = mybir.dt.uint8
 FP8X4 = mybir.dt.float8_e4m3fn_x4
@@ -29,34 +28,30 @@ GROUP_PAIRS = P // (SLOTS * HEADS)
 GROUPS = PAIRS // GROUP_PAIRS
 BLOCK_GROUPS = GROUPS // BLOCKS
 GROUP_COLS = HEADS * GROUP_PAIRS
+PSUM_BANKS = 8
 BANK_F32 = 512
 BANK_GROUPS = BANK_F32 // GROUP_COLS
 ROUNDS = BLOCK_GROUPS // BANK_GROUPS
-PSUM_BANKS = 8
 QUAD = BANK_F32 // BLOCK_PAIRS
-Q_BANKS = SLOTS * HEADS // QUAD
-HALF_COLS = 512
+QUADS = HEADS // QUAD
+HALF_COLS = BANK_F32
 HALF_HEADS = HALF_COLS // D
 HALVES = HEADS // HALF_HEADS
-W_SLOTTED = (2 * HEADS + 1) * D
+
+assert BLOCKS == HALVES * PASSES
 
 FLOPS = 2 * 2 * TOKENS * E * HEADS * D + 2 * TOKENS * HEADS * HEADS * D
 
 
-def head_window(head, slot):
-    first = (2 * head + 1 - slot) * D
-    return slice(first, first + P)
-
-
 def tile_multiheadattention_pa_kernel(tc, x, Wq, Wk, out):
     nc = tc.nc
-    x_blocks = x.flatten_outer_dims().rearrange("(b p s) e -> s b p e", p=P, s=SLOTS)
+    x_blocks = x.flatten_outer_dims().rearrange("(b p s) e -> b s p e", p=P, s=SLOTS)
     out_rows = out.rearrange("n l i j -> (n l i) j").rearrange("(g p) j -> p g j", p=P)
 
     with (
         tc.tile_pool(name="keep", bufs=1) as keep,
         tc.tile_pool(name="w_stage", bufs=3) as w_stage,
-        tc.tile_pool(name="q_pool", bufs=2) as q_pool,
+        tc.tile_pool(name="by_pair", bufs=3) as by_pair,
         tc.tile_pool(name="soft", bufs=4) as soft,
         tc.psum_pool(name="psum", bufs=PSUM_BANKS) as psum,
         tc.manual_schedule(),
@@ -64,10 +59,13 @@ def tile_multiheadattention_pa_kernel(tc, x, Wq, Wk, out):
         identity = keep.tile([P, P], F32)
         make_identity(nc, identity[:])
 
-        x_raw = keep.tile([P, SLOTS, BLOCKS, E], BF16)
-        for slot in range(SLOTS):
-            for block in range(BLOCKS):
-                nc.sync.dma_start(out=x_raw[:, slot, block, :], in_=x_blocks[slot, block])
+        x_raw = keep.tile([P, BLOCKS, SLOTS, E], BF16)
+        wk_raw = keep.tile([P, HALVES, PASSES, PACK, HALF_COLS], BF16)
+        wq_raw = keep.tile([P, HALVES, PASSES, PACK, HALF_COLS], BF16)
+
+        def load_x(block):
+            for slot in range(SLOTS):
+                nc.sync.dma_start(out=x_raw[:, block, slot, :], in_=x_blocks[block, slot])
 
         def load_weight(w, w_raw):
             for half in range(HALVES):
@@ -80,24 +78,32 @@ def tile_multiheadattention_pa_kernel(tc, x, Wq, Wk, out):
                             in_=w[first : first + 2 * P, cols].rearrange("(p r) n -> p r n", r=2),
                         )
 
-        wk_raw = keep.tile([P, HALVES, PASSES, PACK, HALF_COLS], BF16)
-        wq_raw = keep.tile([P, HALVES, PASSES, PACK, HALF_COLS], BF16)
+        load_x(0)
         load_weight(Wk, wk_raw)
+        for block in range(1, BLOCKS):
+            load_x(block)
         load_weight(Wq, wq_raw)
+
+        q_even = keep.tile([P, BLOCK_PAIRS, SLOTS, HEADS], F32)
+        q_odd = keep.tile([P, BLOCK_PAIRS, SLOTS, HEADS], F32)
+        q_stationary = [q_even, q_odd]
+        nc.vector.memset(q_even[:], 0.0)
+        nc.vector.memset(q_odd[:], 0.0)
 
         x_grouped = keep.tile([P, PASSES, SLOTS, PAIRS * PACK], BF16, align_bytes=64)
         x_codes = keep.tile([P, PASSES, SLOTS, PAIRS], U32, align_bytes=64)
         x_scales = keep.tile([P, PASSES, SLOTS, PAIRS], U8, align_bytes=64)
         x_words = x_grouped[:].bitcast(F32).rearrange("p c s (v h) -> p c s v h", h=2)
-        for slot in range(SLOTS):
-            for block in range(BLOCKS):
-                pairs = slice(block * BLOCK_PAIRS, (block + 1) * BLOCK_PAIRS)
-                values = slice(block * BLOCK_PAIRS * PACK, (block + 1) * BLOCK_PAIRS * PACK)
+
+        def quantise_x(block):
+            pairs = slice(block * BLOCK_PAIRS, (block + 1) * BLOCK_PAIRS)
+            values = slice(block * BLOCK_PAIRS * PACK, (block + 1) * BLOCK_PAIRS * PACK)
+            for slot in range(SLOTS):
                 x_t = psum.tile([P, PASSES * 2, BLOCK_PAIRS], F32, tag="bank")
                 for plane in range(PASSES * 2):
                     nc.tensor.transpose(
                         x_t[:, plane, :],
-                        x_raw[:, slot, block, :].bitcast(F32)[:, plane * P : (plane + 1) * P],
+                        x_raw[:, block, slot, :].bitcast(F32)[:, plane * P : (plane + 1) * P],
                         identity[:],
                     )
                 nc.scalar.copy(
@@ -111,89 +117,89 @@ def tile_multiheadattention_pa_kernel(tc, x, Wq, Wk, out):
                         in_=x_grouped[:, c, slot, values],
                     )
 
-        def quantise_weight(w_raw, codes, scales):
-            code_runs = codes[:].bitcast(I32).rearrange("p c (r w) -> p c r w", w=D)
-            scale_runs = scales[:].bitcast(I32).rearrange("p c (r w) -> p c r w", w=D // 4)
-            nc.vector.memset(code_runs[:, :, 0 : 2 * HEADS + 1 : 2, :], 0)
-            nc.vector.memset(scale_runs[:, :, 0 : 2 * HEADS + 1 : 2, :], 0)
-            for half in range(HALVES):
-                grouped = []
-                for c in range(PASSES):
-                    w_grouped = w_stage.tile([P, HALF_COLS, PACK], BF16, align_bytes=64)
-                    nc.vector.tensor_copy(
-                        out=w_grouped[:].rearrange("p (n i) t -> p n t i", i=4),
-                        in_=w_raw[:, half, c].rearrange("p t (n i) -> p n t i", i=4),
-                    )
-                    grouped.append(w_grouped)
-                for h in range(HALF_HEADS):
-                    first = (2 * (half * HALF_HEADS + h) + 1) * D
-                    for c in range(PASSES):
-                        nc.vector.quantize_mx(
-                            out=codes[:, c, first : first + D].bitcast(FP8X4),
-                            scales=scales[:, c, first : first + D],
-                            in_=grouped[c][:, h * D : (h + 1) * D, :].rearrange("p n t -> p (n t)"),
-                        )
+        wk_codes = keep.tile([P, PASSES, HEADS * D], U32, align_bytes=64)
+        wk_scales = keep.tile([P, PASSES, HEADS * D], U8, align_bytes=64)
+        wq_codes = keep.tile([P, PASSES, HEADS * D], U32, align_bytes=64)
+        wq_scales = keep.tile([P, PASSES, HEADS * D], U8, align_bytes=64)
 
-        wk_codes = keep.tile([P, PASSES, W_SLOTTED], U32, align_bytes=64)
-        wk_scales = keep.tile([P, PASSES, W_SLOTTED], U8, align_bytes=64)
-        wq_codes = keep.tile([P, PASSES, W_SLOTTED], U32, align_bytes=64)
-        wq_scales = keep.tile([P, PASSES, W_SLOTTED], U8, align_bytes=64)
-        quantise_weight(wk_raw, wk_codes, wk_scales)
-        quantise_weight(wq_raw, wq_codes, wq_scales)
+        def quantise_weight(w_raw, codes, scales, half, c):
+            cols = slice(half * HALF_COLS, (half + 1) * HALF_COLS)
+            w_grouped = w_stage.tile([P, HALF_COLS, PACK], BF16, align_bytes=64)
+            nc.vector.tensor_copy(
+                out=w_grouped[:].rearrange("p (n i) t -> p n t i", i=4),
+                in_=w_raw[:, half, c].rearrange("p t (n i) -> p n t i", i=4),
+            )
+            nc.vector.quantize_mx(
+                out=codes[:, c, cols].bitcast(FP8X4),
+                scales=scales[:, c, cols],
+                in_=w_grouped[:].rearrange("p n t -> p (n t)"),
+            )
+
+        def project(codes, scales, block):
+            pairs = slice(block * BLOCK_PAIRS, (block + 1) * BLOCK_PAIRS)
+            projected = by_pair.tile([P, HEADS, SLOTS, D], F32)
+            for half in range(HALVES):
+                cols = slice(half * HALF_COLS, (half + 1) * HALF_COLS)
+                for slot in range(SLOTS):
+                    bank = psum.tile([P, HALF_HEADS, D], F32, tag="bank")
+                    for c in range(PASSES):
+                        nc.tensor.matmul_mx(
+                            out=bank[:].rearrange("p i d -> p (i d)"),
+                            lhsT=x_codes[:, c, slot, pairs].bitcast(FP8X4),
+                            lhsT_scale=x_scales[:, c, slot, pairs],
+                            rhs=codes[:, c, cols].bitcast(FP8X4),
+                            rhs_scale=scales[:, c, cols],
+                            start=(c == 0),
+                            stop=(c == PASSES - 1),
+                        )
+                    nc.scalar.copy(
+                        out=projected[:, half * HALF_HEADS : (half + 1) * HALF_HEADS, slot, :], in_=bank[:]
+                    )
+            return projected
+
+        def transpose_heads(projected, quad):
+            bank = psum.tile([P, QUAD, BLOCK_PAIRS], F32, tag="bank")
+            for i in range(QUAD):
+                nc.tensor.transpose(
+                    bank[:, i, :], projected[:, quad * QUAD + i].rearrange("p s d -> p (s d)"), identity[:]
+                )
+            return bank
 
         k_moving = keep.tile([P, GROUPS, HEADS, GROUP_PAIRS], F32)
-        for head in range(HEADS):
-            k_bank = psum.tile([P, PAIRS], F32, tag="bank")
-            for c in range(PASSES):
-                for slot in range(SLOTS):
-                    nc.tensor.matmul_mx(
-                        out=k_bank[:],
-                        lhsT=wk_codes[:, c, head_window(head, slot)].bitcast(FP8X4),
-                        lhsT_scale=wk_scales[:, c, head_window(head, slot)],
-                        rhs=x_codes[:, c, slot, :].bitcast(FP8X4),
-                        rhs_scale=x_scales[:, c, slot, :],
-                        start=(c == 0 and slot == 0),
-                        stop=(c == PASSES - 1 and slot == SLOTS - 1),
-                    )
-            nc.scalar.copy(
-                out=k_moving[:, :, head, :],
-                in_=k_bank[:].rearrange("p (g v) -> p g v", v=GROUP_PAIRS),
-            )
 
-        def new_q():
-            q_stationary = q_pool.tile([P, BLOCK_PAIRS, SLOTS, HEADS], F32)
-            return q_stationary
+        def transpose_k(projected, block):
+            groups = slice(block * BLOCK_GROUPS, (block + 1) * BLOCK_GROUPS)
+            for quad in range(QUADS):
+                bank = transpose_heads(projected, quad)
+                k_out = k_moving[:, groups, quad * QUAD : (quad + 1) * QUAD, :]
+                k_in = bank[:].rearrange("p j (g v) -> p g j v", v=GROUP_PAIRS)
+                if quad % 2 == 0:
+                    nc.scalar.copy(out=k_out, in_=k_in)
+                else:
+                    nc.vector.tensor_copy(out=k_out, in_=k_in)
 
-        def project_q(block, bank, q_stationary):
-            slot, quad = divmod(bank, HEADS // QUAD)
-            pairs = slice(block * BLOCK_PAIRS, (block + 1) * BLOCK_PAIRS)
-            q_bank = psum.tile([P, QUAD, BLOCK_PAIRS], F32, tag="bank")
-            for i in range(QUAD):
-                head = quad * QUAD + i
-                for c in range(PASSES):
-                    nc.tensor.matmul_mx(
-                        out=q_bank[:, i, :],
-                        lhsT=wq_codes[:, c, head_window(head, slot)].bitcast(FP8X4),
-                        lhsT_scale=wq_scales[:, c, head_window(head, slot)],
-                        rhs=x_codes[:, c, slot, pairs].bitcast(FP8X4),
-                        rhs_scale=x_scales[:, c, slot, pairs],
-                        start=(c == 0),
-                        stop=(c == PASSES - 1),
-                    )
-            nc.scalar.copy(
-                out=q_stationary[:, :, slot, quad * QUAD : (quad + 1) * QUAD],
-                in_=q_bank[:].rearrange("p i v -> p v i"),
-            )
+        def transpose_q(projected, block):
+            q_tile = q_stationary[block % 2]
+            for quad in range(QUADS):
+                bank = transpose_heads(projected, quad)
+                heads = slice(quad * QUAD, (quad + 1) * QUAD)
+                nc.scalar.copy(
+                    out=q_tile[0:D, :, 0, heads], in_=bank[0:D, :, :].rearrange("p i v -> p v i")
+                )
+                nc.vector.tensor_copy(
+                    out=q_tile[D:P, :, 1, heads], in_=bank[D:P, :, :].rearrange("p i v -> p v i")
+                )
 
         wide = [P, BANK_GROUPS, HEADS]
 
-        def shifted_scores(block, r, q_stationary):
+        def shifted_scores(block, r):
+            q_tile = q_stationary[block % 2]
             e_bank = psum.tile([P, BANK_GROUPS, HEADS, GROUP_PAIRS], F32, tag="bank")
             for g in range(BANK_GROUPS):
                 local = r * BANK_GROUPS + g
                 nc.tensor.matmul(
                     out=e_bank[:, g].rearrange("p j v -> p (j v)"),
-                    lhsT=q_stationary[:, local * GROUP_PAIRS : (local + 1) * GROUP_PAIRS].rearrange(
+                    lhsT=q_tile[:, local * GROUP_PAIRS : (local + 1) * GROUP_PAIRS].rearrange(
                         "p u s i -> p (u s i)"
                     ),
                     rhs=k_moving[:, block * BLOCK_GROUPS + local].rearrange("p j v -> p (j v)"),
@@ -226,21 +232,35 @@ def tile_multiheadattention_pa_kernel(tc, x, Wq, Wk, out):
             first = block * BLOCK_GROUPS + r * BANK_GROUPS
             nc.sync.dma_start(out=out_rows[:, first : first + BANK_GROUPS, :], in_=weights[:])
 
-        q_next = new_q()
-        for bank in range(Q_BANKS):
-            project_q(0, bank, q_next)
+        quantise_x(0)
+        for half in range(HALVES):
+            for c in range(PASSES):
+                quantise_weight(wk_raw, wk_codes, wk_scales, half, c)
+        for block in range(1, BLOCKS):
+            quantise_x(block)
+
+        k_waiting = []
+        for block in range(BLOCKS):
+            k_projected = project(wk_codes, wk_scales, block)
+            for earlier in k_waiting:
+                transpose_k(*earlier)
+            k_waiting = [(k_projected, block)]
+            quantise_weight(wq_raw, wq_codes, wq_scales, block // PASSES, block % PASSES)
+        q_projected = project(wq_codes, wq_scales, 0)
+        for earlier in k_waiting:
+            transpose_k(*earlier)
+        transpose_q(q_projected, 0)
+
         unfinished = []
         for block in range(BLOCKS):
-            q_now = q_next
-            if block + 1 < BLOCKS:
-                q_next = new_q()
             for r in range(ROUNDS):
-                if block + 1 < BLOCKS:
-                    for bank in range(r * Q_BANKS // ROUNDS, (r + 1) * Q_BANKS // ROUNDS):
-                        project_q(block + 1, bank, q_next)
-                scores = shifted_scores(block, r, q_now)
+                scores = shifted_scores(block, r)
                 for earlier in unfinished:
                     normalise_and_store(*earlier)
                 unfinished = [(block, r, scores)]
+                if block + 1 < BLOCKS and r == 0:
+                    q_projected = project(wq_codes, wq_scales, block + 1)
+                if block + 1 < BLOCKS and r == 1:
+                    transpose_q(q_projected, block + 1)
         for earlier in unfinished:
             normalise_and_store(*earlier)

@@ -32,13 +32,13 @@ PSUM_BANKS = 8
 BANK_F32 = 512
 BANK_GROUPS = BANK_F32 // GROUP_COLS
 ROUNDS = BLOCK_GROUPS // BANK_GROUPS
+BATCH = 2
+BATCH_GROUPS = BATCH * BANK_GROUPS
 QUAD = BANK_F32 // BLOCK_PAIRS
-QUADS = HEADS // QUAD
 HALF_COLS = BANK_F32
 HALF_HEADS = HALF_COLS // D
 HALVES = HEADS // HALF_HEADS
-
-assert BLOCKS == HALVES * PASSES
+HALF_QUADS = HALF_HEADS // QUAD
 
 FLOPS = 2 * 2 * TOKENS * E * HEADS * D + 2 * TOKENS * HEADS * HEADS * D
 
@@ -51,7 +51,7 @@ def tile_multiheadattention_pa_kernel(tc, x, Wq, Wk, out):
     with (
         tc.tile_pool(name="keep", bufs=1) as keep,
         tc.tile_pool(name="w_stage", bufs=3) as w_stage,
-        tc.tile_pool(name="by_pair", bufs=3) as by_pair,
+        tc.tile_pool(name="by_pair", bufs=4) as by_pair,
         tc.tile_pool(name="soft", bufs=4) as soft,
         tc.psum_pool(name="psum", bufs=PSUM_BANKS) as psum,
         tc.manual_schedule(),
@@ -67,22 +67,23 @@ def tile_multiheadattention_pa_kernel(tc, x, Wq, Wk, out):
             for slot in range(SLOTS):
                 nc.sync.dma_start(out=x_raw[:, block, slot, :], in_=x_blocks[block, slot])
 
-        def load_weight(w, w_raw):
-            for half in range(HALVES):
-                cols = slice(half * HALF_COLS, (half + 1) * HALF_COLS)
-                for c in range(PASSES):
-                    for h in range(2):
-                        first = c * K_PASS + h * 2 * P
-                        nc.sync.dma_start(
-                            out=w_raw[:, half, c, 2 * h : 2 * h + 2, :],
-                            in_=w[first : first + 2 * P, cols].rearrange("(p r) n -> p r n", r=2),
-                        )
+        def load_weight(w, w_raw, half):
+            cols = slice(half * HALF_COLS, (half + 1) * HALF_COLS)
+            for c in range(PASSES):
+                for h in range(2):
+                    first = c * K_PASS + h * 2 * P
+                    nc.sync.dma_start(
+                        out=w_raw[:, half, c, 2 * h : 2 * h + 2, :],
+                        in_=w[first : first + 2 * P, cols].rearrange("(p r) n -> p r n", r=2),
+                    )
 
         load_x(0)
-        load_weight(Wk, wk_raw)
+        load_weight(Wk, wk_raw, 0)
         for block in range(1, BLOCKS):
             load_x(block)
-        load_weight(Wq, wq_raw)
+        load_weight(Wk, wk_raw, 1)
+        load_weight(Wq, wq_raw, 0)
+        load_weight(Wq, wq_raw, 1)
 
         q_even = keep.tile([P, BLOCK_PAIRS, SLOTS, HEADS], F32)
         q_odd = keep.tile([P, BLOCK_PAIRS, SLOTS, HEADS], F32)
@@ -122,39 +123,40 @@ def tile_multiheadattention_pa_kernel(tc, x, Wq, Wk, out):
         wq_codes = keep.tile([P, PASSES, HEADS * D], U32, align_bytes=64)
         wq_scales = keep.tile([P, PASSES, HEADS * D], U8, align_bytes=64)
 
-        def quantise_weight(w_raw, codes, scales, half, c):
+        def quantise_weight(w_raw, codes, scales, half):
             cols = slice(half * HALF_COLS, (half + 1) * HALF_COLS)
-            w_grouped = w_stage.tile([P, HALF_COLS, PACK], BF16, align_bytes=64)
-            nc.vector.tensor_copy(
-                out=w_grouped[:].rearrange("p (n i) t -> p n t i", i=4),
-                in_=w_raw[:, half, c].rearrange("p t (n i) -> p n t i", i=4),
-            )
-            nc.vector.quantize_mx(
-                out=codes[:, c, cols].bitcast(FP8X4),
-                scales=scales[:, c, cols],
-                in_=w_grouped[:].rearrange("p n t -> p (n t)"),
-            )
+            grouped = []
+            for c in range(PASSES):
+                w_grouped = w_stage.tile([P, HALF_COLS, PACK], BF16, align_bytes=64)
+                nc.vector.tensor_copy(
+                    out=w_grouped[:].rearrange("p (n i) t -> p n t i", i=4),
+                    in_=w_raw[:, half, c].rearrange("p t (n i) -> p n t i", i=4),
+                )
+                grouped.append(w_grouped)
+            for c in range(PASSES):
+                nc.vector.quantize_mx(
+                    out=codes[:, c, cols].bitcast(FP8X4),
+                    scales=scales[:, c, cols],
+                    in_=grouped[c][:].rearrange("p n t -> p (n t)"),
+                )
 
-        def project(codes, scales, block):
+        def project(codes, scales, half, block):
             pairs = slice(block * BLOCK_PAIRS, (block + 1) * BLOCK_PAIRS)
-            projected = by_pair.tile([P, HEADS, SLOTS, D], F32)
-            for half in range(HALVES):
-                cols = slice(half * HALF_COLS, (half + 1) * HALF_COLS)
-                for slot in range(SLOTS):
-                    bank = psum.tile([P, HALF_HEADS, D], F32, tag="bank")
-                    for c in range(PASSES):
-                        nc.tensor.matmul_mx(
-                            out=bank[:].rearrange("p i d -> p (i d)"),
-                            lhsT=x_codes[:, c, slot, pairs].bitcast(FP8X4),
-                            lhsT_scale=x_scales[:, c, slot, pairs],
-                            rhs=codes[:, c, cols].bitcast(FP8X4),
-                            rhs_scale=scales[:, c, cols],
-                            start=(c == 0),
-                            stop=(c == PASSES - 1),
-                        )
-                    nc.scalar.copy(
-                        out=projected[:, half * HALF_HEADS : (half + 1) * HALF_HEADS, slot, :], in_=bank[:]
+            cols = slice(half * HALF_COLS, (half + 1) * HALF_COLS)
+            projected = by_pair.tile([P, HALF_HEADS, SLOTS, D], F32)
+            for slot in range(SLOTS):
+                bank = psum.tile([P, HALF_HEADS, D], F32, tag="bank")
+                for c in range(PASSES):
+                    nc.tensor.matmul_mx(
+                        out=bank[:].rearrange("p i d -> p (i d)"),
+                        lhsT=x_codes[:, c, slot, pairs].bitcast(FP8X4),
+                        lhsT_scale=x_scales[:, c, slot, pairs],
+                        rhs=codes[:, c, cols].bitcast(FP8X4),
+                        rhs_scale=scales[:, c, cols],
+                        start=(c == 0),
+                        stop=(c == PASSES - 1),
                     )
+                nc.scalar.copy(out=projected[:, :, slot, :], in_=bank[:])
             return projected
 
         def transpose_heads(projected, quad):
@@ -167,22 +169,24 @@ def tile_multiheadattention_pa_kernel(tc, x, Wq, Wk, out):
 
         k_moving = keep.tile([P, GROUPS, HEADS, GROUP_PAIRS], F32)
 
-        def transpose_k(projected, block):
+        def transpose_k(projected, half, block):
             groups = slice(block * BLOCK_GROUPS, (block + 1) * BLOCK_GROUPS)
-            for quad in range(QUADS):
+            for quad in range(HALF_QUADS):
                 bank = transpose_heads(projected, quad)
-                k_out = k_moving[:, groups, quad * QUAD : (quad + 1) * QUAD, :]
+                first = half * HALF_HEADS + quad * QUAD
+                k_out = k_moving[:, groups, first : first + QUAD, :]
                 k_in = bank[:].rearrange("p j (g v) -> p g j v", v=GROUP_PAIRS)
-                if quad % 2 == 0:
+                if half == 0:
                     nc.scalar.copy(out=k_out, in_=k_in)
                 else:
                     nc.vector.tensor_copy(out=k_out, in_=k_in)
 
-        def transpose_q(projected, block):
+        def transpose_q(projected, half, block):
             q_tile = q_stationary[block % 2]
-            for quad in range(QUADS):
+            for quad in range(HALF_QUADS):
                 bank = transpose_heads(projected, quad)
-                heads = slice(quad * QUAD, (quad + 1) * QUAD)
+                first = half * HALF_HEADS + quad * QUAD
+                heads = slice(first, first + QUAD)
                 nc.scalar.copy(
                     out=q_tile[0:D, :, 0, heads], in_=bank[0:D, :, :].rearrange("p i v -> p v i")
                 )
@@ -190,9 +194,7 @@ def tile_multiheadattention_pa_kernel(tc, x, Wq, Wk, out):
                     out=q_tile[D:P, :, 1, heads], in_=bank[D:P, :, :].rearrange("p i v -> p v i")
                 )
 
-        wide = [P, BANK_GROUPS, HEADS]
-
-        def shifted_scores(block, r):
+        def energies(block, r, scores):
             q_tile = q_stationary[block % 2]
             e_bank = psum.tile([P, BANK_GROUPS, HEADS, GROUP_PAIRS], F32, tag="bank")
             for g in range(BANK_GROUPS):
@@ -206,61 +208,71 @@ def tile_multiheadattention_pa_kernel(tc, x, Wq, Wk, out):
                     start=True,
                     stop=True,
                 )
-            scores = soft.tile(wide, F32)
+            kept = slice((r % BATCH) * BANK_GROUPS, (r % BATCH + 1) * BANK_GROUPS)
             for u in range(GROUP_PAIRS):
                 rows = slice(u * SLOTS * HEADS, (u + 1) * SLOTS * HEADS)
                 if u % 2 == 0:
-                    nc.scalar.copy(out=scores[rows, :, :], in_=e_bank[rows, :, :, u])
+                    nc.scalar.copy(out=scores[rows, kept, :], in_=e_bank[rows, :, :, u])
                 else:
-                    nc.vector.tensor_copy(out=scores[rows, :, :], in_=e_bank[rows, :, :, u])
-            top = soft.tile([P, BANK_GROUPS], F32)
+                    nc.vector.tensor_copy(out=scores[rows, kept, :], in_=e_bank[rows, :, :, u])
+
+        wide = [P, BATCH_GROUPS, HEADS]
+
+        def subtract_max(scores):
+            top = soft.tile([P, BATCH_GROUPS], F32)
             nc.vector.tensor_reduce(out=top[:], in_=scores[:], axis=AXIS_X, op=ALU.max)
             nc.vector.tensor_tensor(
                 out=scores[:], in0=scores[:], in1=top[:].unsqueeze(2).to_broadcast(wide), op=ALU.subtract
             )
-            return scores
 
-        def normalise_and_store(block, r, scores):
+        def normalise_and_store(first, scores):
             weights = soft.tile(wide, F32)
             nc.scalar.activation(out=weights[:], in_=scores[:], func=ACT.Exp, scale=1.0 / math.sqrt(E))
-            total = soft.tile([P, BANK_GROUPS], F32)
+            total = soft.tile([P, BATCH_GROUPS], F32)
             nc.vector.tensor_reduce(out=total[:], in_=weights[:], axis=AXIS_X, op=ALU.add)
             nc.vector.reciprocal(out=total[:], in_=total[:])
             nc.vector.tensor_tensor(
                 out=weights[:], in0=weights[:], in1=total[:].unsqueeze(2).to_broadcast(wide), op=ALU.mult
             )
-            first = block * BLOCK_GROUPS + r * BANK_GROUPS
-            nc.sync.dma_start(out=out_rows[:, first : first + BANK_GROUPS, :], in_=weights[:])
+            nc.sync.dma_start(out=out_rows[:, first : first + BATCH_GROUPS, :], in_=weights[:])
 
         quantise_x(0)
-        for half in range(HALVES):
-            for c in range(PASSES):
-                quantise_weight(wk_raw, wk_codes, wk_scales, half, c)
+        quantise_weight(wk_raw, wk_codes, wk_scales, 0)
         for block in range(1, BLOCKS):
             quantise_x(block)
+        quantise_weight(wk_raw, wk_codes, wk_scales, 1)
+        quantise_weight(wq_raw, wq_codes, wq_scales, 0)
+        quantise_weight(wq_raw, wq_codes, wq_scales, 1)
 
-        k_waiting = []
-        for block in range(BLOCKS):
-            k_projected = project(wk_codes, wk_scales, block)
-            for earlier in k_waiting:
-                transpose_k(*earlier)
-            k_waiting = [(k_projected, block)]
-            quantise_weight(wq_raw, wq_codes, wq_scales, block // PASSES, block % PASSES)
-        q_projected = project(wq_codes, wq_scales, 0)
-        for earlier in k_waiting:
+        waiting = []
+        for half in range(HALVES):
+            for block in range(BLOCKS):
+                projected = project(wk_codes, wk_scales, half, block)
+                for earlier in waiting:
+                    transpose_k(*earlier)
+                waiting = [(projected, half, block)]
+        q_halves = [project(wq_codes, wq_scales, 0, 0)]
+        for earlier in waiting:
             transpose_k(*earlier)
-        transpose_q(q_projected, 0)
+        q_halves.append(project(wq_codes, wq_scales, 1, 0))
+        for half in range(HALVES):
+            transpose_q(q_halves[half], half, 0)
 
         unfinished = []
         for block in range(BLOCKS):
             for r in range(ROUNDS):
-                scores = shifted_scores(block, r)
-                for earlier in unfinished:
-                    normalise_and_store(*earlier)
-                unfinished = [(block, r, scores)]
+                if r % BATCH == 0:
+                    scores = soft.tile(wide, F32)
+                energies(block, r, scores)
+                if r % BATCH == BATCH - 1:
+                    subtract_max(scores)
+                    for earlier in unfinished:
+                        normalise_and_store(*earlier)
+                    unfinished = [(block * BLOCK_GROUPS + (r - BATCH + 1) * BANK_GROUPS, scores)]
                 if block + 1 < BLOCKS and r == 0:
-                    q_projected = project(wq_codes, wq_scales, block + 1)
+                    q_halves = [project(wq_codes, wq_scales, half, block + 1) for half in range(HALVES)]
                 if block + 1 < BLOCKS and r == 1:
-                    transpose_q(q_projected, block + 1)
+                    for half in range(HALVES):
+                        transpose_q(q_halves[half], half, block + 1)
         for earlier in unfinished:
             normalise_and_store(*earlier)

import math

import concourse.mybir as mybir
from concourse.masks import make_identity

F32 = mybir.dt.float32
BF16 = mybir.dt.bfloat16
U32 = mybir.dt.uint32
U8 = mybir.dt.uint8
FP8X4 = mybir.dt.float8_e4m3fn_x4
ALU = mybir.AluOpType
ACT = mybir.ActivationFunctionType
AXIS_X = mybir.AxisListType.X

P = 128
PACK = 4
K_PASS = P * PACK
TOKENS = 4 * 256
E = 1024
HEADS = 16
D = 64
PASSES = E // K_PASS
SLOTS = 2
PAIRS = TOKENS // SLOTS
BLOCK_PAIRS = P
BLOCKS = PAIRS // BLOCK_PAIRS
GROUP_PAIRS = P // (SLOTS * HEADS)
GROUPS = PAIRS // GROUP_PAIRS
BLOCK_GROUPS = GROUPS // BLOCKS
GROUP_COLS = HEADS * GROUP_PAIRS
PSUM_BANKS = 8
BANK_F32 = 512
BANK_GROUPS = BANK_F32 // GROUP_COLS
ROUNDS = BLOCK_GROUPS // BANK_GROUPS
BATCH = 2
BATCH_GROUPS = BATCH * BANK_GROUPS
QUAD = BANK_F32 // BLOCK_PAIRS
HALF_COLS = BANK_F32
HALF_HEADS = HALF_COLS // D
HALVES = HEADS // HALF_HEADS
HALF_QUADS = HALF_HEADS // QUAD

FLOPS = 2 * 2 * TOKENS * E * HEADS * D + 2 * TOKENS * HEADS * HEADS * D


def tile_multiheadattention_pa_kernel(tc, x, Wq, Wk, out):
    nc = tc.nc
    x_blocks = x.flatten_outer_dims().rearrange("(b p s) e -> b s p e", p=P, s=SLOTS)
    out_rows = out.rearrange("n l i j -> (n l i) j").rearrange("(g p) j -> p g j", p=P)

    with (
        tc.tile_pool(name="keep", bufs=1) as keep,
        tc.tile_pool(name="w_stage", bufs=3) as w_stage,
        tc.tile_pool(name="by_pair", bufs=4) as by_pair,
        tc.tile_pool(name="soft", bufs=4) as soft,
        tc.psum_pool(name="psum", bufs=PSUM_BANKS) as psum,
        tc.manual_schedule(),
    ):
        identity = keep.tile([P, P], F32)
        make_identity(nc, identity[:])

        x_raw = keep.tile([P, BLOCKS, SLOTS, E], BF16)
        wk_raw = keep.tile([P, HALVES, PASSES, PACK, HALF_COLS], BF16)
        wq_raw = keep.tile([P, HALVES, PASSES, PACK, HALF_COLS], BF16)

        def load_x(block):
            for slot in range(SLOTS):
                nc.sync.dma_start(out=x_raw[:, block, slot, :], in_=x_blocks[block, slot])

        def load_weight(w, w_raw, half):
            cols = slice(half * HALF_COLS, (half + 1) * HALF_COLS)
            for c in range(PASSES):
                for h in range(2):
                    first = c * K_PASS + h * 2 * P
                    nc.sync.dma_start(
                        out=w_raw[:, half, c, 2 * h : 2 * h + 2, :],
                        in_=w[first : first + 2 * P, cols].rearrange("(p r) n -> p r n", r=2),
                    )

        load_x(0)
        load_weight(Wk, wk_raw, 0)
        for block in range(1, BLOCKS):
            load_x(block)
        load_weight(Wk, wk_raw, 1)
        load_weight(Wq, wq_raw, 0)
        load_weight(Wq, wq_raw, 1)

        q_even = keep.tile([P, BLOCK_PAIRS, SLOTS, HEADS], F32)
        q_odd = keep.tile([P, BLOCK_PAIRS, SLOTS, HEADS], F32)
        q_stationary = [q_even, q_odd]
        nc.vector.memset(q_even[:], 0.0)
        nc.vector.memset(q_odd[:], 0.0)

        x_grouped = keep.tile([P, PASSES, SLOTS, PAIRS * PACK], BF16, align_bytes=64)
        x_codes = keep.tile([P, PASSES, SLOTS, PAIRS], U32, align_bytes=64)
        x_scales = keep.tile([P, PASSES, SLOTS, PAIRS], U8, align_bytes=64)
        x_words = x_grouped[:].bitcast(F32).rearrange("p c s (v h) -> p c s v h", h=2)

        def quantise_x(block):
            pairs = slice(block * BLOCK_PAIRS, (block + 1) * BLOCK_PAIRS)
            values = slice(block * BLOCK_PAIRS * PACK, (block + 1) * BLOCK_PAIRS * PACK)
            for slot in range(SLOTS):
                x_t = psum.tile([P, PASSES * 2, BLOCK_PAIRS], F32, tag="bank")
                for plane in range(PASSES * 2):
                    nc.tensor.transpose(
                        x_t[:, plane, :],
                        x_raw[:, block, slot, :].bitcast(F32)[:, plane * P : (plane + 1) * P],
                        identity[:],
                    )
                nc.scalar.copy(
                    out=x_words[:, :, slot, pairs, :],
                    in_=x_t[:].rearrange("p (c h) v -> p c v h", h=2),
                )
                for c in range(PASSES):
                    nc.vector.quantize_mx(
                        out=x_codes[:, c, slot, pairs].bitcast(FP8X4),
                        scales=x_scales[:, c, slot, pairs],
                        in_=x_grouped[:, c, slot, values],
                    )

        wk_codes = keep.tile([P, PASSES, HEADS * D], U32, align_bytes=64)
        wk_scales = keep.tile([P, PASSES, HEADS * D], U8, align_bytes=64)
        wq_codes = keep.tile([P, PASSES, HEADS * D], U32, align_bytes=64)
        wq_scales = keep.tile([P, PASSES, HEADS * D], U8, align_bytes=64)

        def quantise_weight(w_raw, codes, scales, half):
            cols = slice(half * HALF_COLS, (half + 1) * HALF_COLS)
            grouped = []
            for c in range(PASSES):
                w_grouped = w_stage.tile([P, HALF_COLS, PACK], BF16, align_bytes=64)
                nc.vector.tensor_copy(
                    out=w_grouped[:].rearrange("p (n i) t -> p n t i", i=4),
                    in_=w_raw[:, half, c].rearrange("p t (n i) -> p n t i", i=4),
                )
                grouped.append(w_grouped)
            for c in range(PASSES):
                nc.vector.quantize_mx(
                    out=codes[:, c, cols].bitcast(FP8X4),
                    scales=scales[:, c, cols],
                    in_=grouped[c][:].rearrange("p n t -> p (n t)"),
                )

        def project(codes, scales, half, block):
            pairs = slice(block * BLOCK_PAIRS, (block + 1) * BLOCK_PAIRS)
            cols = slice(half * HALF_COLS, (half + 1) * HALF_COLS)
            projected = by_pair.tile([P, HALF_HEADS, SLOTS, D], F32)
            for slot in range(SLOTS):
                bank = psum.tile([P, HALF_HEADS, D], F32, tag="bank")
                for c in range(PASSES):
                    nc.tensor.matmul_mx(
                        out=bank[:].rearrange("p i d -> p (i d)"),
                        lhsT=x_codes[:, c, slot, pairs].bitcast(FP8X4),
                        lhsT_scale=x_scales[:, c, slot, pairs],
                        rhs=codes[:, c, cols].bitcast(FP8X4),
                        rhs_scale=scales[:, c, cols],
                        start=(c == 0),
                        stop=(c == PASSES - 1),
                    )
                nc.scalar.copy(out=projected[:, :, slot, :], in_=bank[:])
            return projected

        def transpose_heads(projected, quad):
            bank = psum.tile([P, QUAD, BLOCK_PAIRS], F32, tag="bank")
            for i in range(QUAD):
                nc.tensor.transpose(
                    bank[:, i, :], projected[:, quad * QUAD + i].rearrange("p s d -> p (s d)"), identity[:]
                )
            return bank

        k_moving = keep.tile([P, GROUPS, HEADS, GROUP_PAIRS], F32)

        def transpose_k(projected, half, block):
            groups = slice(block * BLOCK_GROUPS, (block + 1) * BLOCK_GROUPS)
            for quad in range(HALF_QUADS):
                bank = transpose_heads(projected, quad)
                first = half * HALF_HEADS + quad * QUAD
                k_out = k_moving[:, groups, first : first + QUAD, :]
                k_in = bank[:].rearrange("p j (g v) -> p g j v", v=GROUP_PAIRS)
                if half == 0:
                    nc.scalar.copy(out=k_out, in_=k_in)
                else:
                    nc.vector.tensor_copy(out=k_out, in_=k_in)

        def transpose_q(projected, half, block):
            q_tile = q_stationary[block % 2]
            for quad in range(HALF_QUADS):
                bank = transpose_heads(projected, quad)
                first = half * HALF_HEADS + quad * QUAD
                heads = slice(first, first + QUAD)
                nc.scalar.copy(
                    out=q_tile[0:D, :, 0, heads], in_=bank[0:D, :, :].rearrange("p i v -> p v i")
                )
                nc.vector.tensor_copy(
                    out=q_tile[D:P, :, 1, heads], in_=bank[D:P, :, :].rearrange("p i v -> p v i")
                )

        def energies(block, r, scores):
            q_tile = q_stationary[block % 2]
            e_bank = psum.tile([P, BANK_GROUPS, HEADS, GROUP_PAIRS], F32, tag="bank")
            for g in range(BANK_GROUPS):
                local = r * BANK_GROUPS + g
                nc.tensor.matmul(
                    out=e_bank[:, g].rearrange("p j v -> p (j v)"),
                    lhsT=q_tile[:, local * GROUP_PAIRS : (local + 1) * GROUP_PAIRS].rearrange(
                        "p u s i -> p (u s i)"
                    ),
                    rhs=k_moving[:, block * BLOCK_GROUPS + local].rearrange("p j v -> p (j v)"),
                    start=True,
                    stop=True,
                )
            kept = slice((r % BATCH) * BANK_GROUPS, (r % BATCH + 1) * BANK_GROUPS)
            for u in range(GROUP_PAIRS):
                rows = slice(u * SLOTS * HEADS, (u + 1) * SLOTS * HEADS)
                if u % 2 == 0:
                    nc.scalar.copy(out=scores[rows, kept, :], in_=e_bank[rows, :, :, u])
                else:
                    nc.vector.tensor_copy(out=scores[rows, kept, :], in_=e_bank[rows, :, :, u])

        wide = [P, BATCH_GROUPS, HEADS]

        def subtract_max(scores):
            top = soft.tile([P, BATCH_GROUPS], F32)
            nc.vector.tensor_reduce(out=top[:], in_=scores[:], axis=AXIS_X, op=ALU.max)
            nc.vector.tensor_tensor(
                out=scores[:], in0=scores[:], in1=top[:].unsqueeze(2).to_broadcast(wide), op=ALU.subtract
            )

        def normalise_and_store(first, scores):
            weights = soft.tile(wide, F32)
            nc.scalar.activation(out=weights[:], in_=scores[:], func=ACT.Exp, scale=1.0 / math.sqrt(E))
            total = soft.tile([P, BATCH_GROUPS], F32)
            nc.vector.tensor_reduce(out=total[:], in_=weights[:], axis=AXIS_X, op=ALU.add)
            nc.vector.reciprocal(out=total[:], in_=total[:])
            nc.vector.tensor_tensor(
                out=weights[:], in0=weights[:], in1=total[:].unsqueeze(2).to_broadcast(wide), op=ALU.mult
            )
            nc.sync.dma_start(out=out_rows[:, first : first + BATCH_GROUPS, :], in_=weights[:])

        quantise_x(0)
        quantise_weight(wk_raw, wk_codes, wk_scales, 0)
        for block in range(1, BLOCKS):
            quantise_x(block)
        quantise_weight(wk_raw, wk_codes, wk_scales, 1)
        quantise_weight(wq_raw, wq_codes, wq_scales, 0)
        quantise_weight(wq_raw, wq_codes, wq_scales, 1)

        waiting = []
        for half in range(HALVES):
            for block in range(BLOCKS):
                projected = project(wk_codes, wk_scales, half, block)
                for earlier in waiting:
                    transpose_k(*earlier)
                waiting = [(projected, half, block)]
        q_halves = [project(wq_codes, wq_scales, 0, 0)]
        for earlier in waiting:
            transpose_k(*earlier)
        q_halves.append(project(wq_codes, wq_scales, 1, 0))
        for half in range(HALVES):
            transpose_q(q_halves[half], half, 0)

        unfinished = []
        for block in range(BLOCKS):
            for r in range(ROUNDS):
                if r % BATCH == 0:
                    scores = soft.tile(wide, F32)
                energies(block, r, scores)
                if r % BATCH == BATCH - 1:
                    subtract_max(scores)
                    for earlier in unfinished:
                        normalise_and_store(*earlier)
                    unfinished = [(block * BLOCK_GROUPS + (r - BATCH + 1) * BANK_GROUPS, scores)]
                if block + 1 < BLOCKS and r == 0:
                    q_halves = [project(wq_codes, wq_scales, half, block + 1) for half in range(HALVES)]
                if block + 1 < BLOCKS and r == 1:
                    for half in range(HALVES):
                        transpose_q(q_halves[half], half, block + 1)
        for earlier in unfinished:
            normalise_and_store(*earlier)
